import numpy as np
import ml_dtypes


def mxq(x, axis, fmt="e4m3"):
    dtype, down = {"e4m3": (ml_dtypes.float8_e4m3fn, 7), "e5m2": (ml_dtypes.float8_e5m2, 14)}[fmt]
    v = np.moveaxis(np.asarray(x, np.float32).astype(ml_dtypes.bfloat16).astype(np.float64), axis, -1)
    blocks = v.reshape(v.shape[:-1] + (-1, 32))
    amax = np.abs(blocks).max(-1, keepdims=True)
    byte = np.maximum(np.where(amax > 0, np.frexp(amax)[1] - 1 + 127, 0) - down, 1)
    scale = np.exp2(byte - 127.0)
    codes = (blocks / scale).astype(np.float32).astype(dtype).astype(np.float64)
    return np.moveaxis((codes * scale).reshape(v.shape), -1, axis)


WIDE = False


def mx_kscale(k):
    if not WIDE:
        return np.ones(k)
    levels = np.array([10, -10, 5, -5, 0])
    a = np.random.permutation(np.resize(levels, k // 512 * 4)).reshape(k // 512, 4)
    idx = np.arange(k)
    return np.exp2(a[idx // 512, idx % 128 // 32])


BF16 = ml_dtypes.bfloat16


def bf(x):
    return np.asarray(x, np.float32).astype(BF16)


def f64(x):
    return np.asarray(x).astype(np.float64)


N, H0C, W0C, H1C, W1C, C = 1, 32, 32, 32, 32, 512
L, S = H0C * W0C, H1C * W1C
P = max(L, S)
THR = 0.2
BORDER = 2
TEMP_INIT = 10.0


def softmax(v, axis):
    e = np.exp(v - v.max(axis=axis, keepdims=True))
    return e / e.sum(axis=axis, keepdims=True)


def border_mask():
    def ok(n):
        a = np.arange(n)
        return (a >= BORDER) & (a < n - BORDER)
    m = (ok(H0C)[:, None, None, None] & ok(W0C)[None, :, None, None]
         & ok(H1C)[None, None, :, None] & ok(W1C)[None, None, None, :])
    return m.reshape(L, S)


def setup_inputs():
    s = mx_kscale(C)
    g = np.random.standard_normal((N, P, C))
    i0 = np.random.randint(0, P, (N, L))
    i1 = np.random.randint(0, P, (N, S))
    n = np.arange(N)[:, None]
    c0 = np.sqrt(0.9) * g[n, i0] + np.sqrt(0.1) * np.random.standard_normal((N, L, C))
    c1 = np.sqrt(0.9) * g[n, i1] + np.sqrt(0.1) * np.random.standard_normal((N, S, C))
    return {"feat_c0": bf(c0 * s), "feat_c1": bf(c1 / s),
            "temperature": bf(TEMP_INIT * (1.0 + 0.03 * np.random.standard_normal(1)))}


def reference(feat_c0, feat_c1, temperature):
    inv_sqrt_c = 1.0 / float(C) ** 0.5
    f0 = f64(feat_c0) * inv_sqrt_c
    f1 = f64(feat_c1) * inv_sqrt_c
    sim = (mxq(f0, 2, "e4m3") @ mxq(f1, 2, "e4m3").transpose(0, 2, 1)) * f64(temperature)
    conf = softmax(sim, 1) * softmax(sim, 2)
    mask = (conf > THR) & border_mask()[None]
    mutual = (mask
              & (conf == conf.max(axis=2, keepdims=True))
              & (conf == conf.max(axis=1, keepdims=True)))
    mconf = np.where(mutual, conf, 0.0)
    return conf, mconf

@@ -1,0 +1,280 @@
+from contextlib import ExitStack
+
+import concourse.mybir as mybir
+from concourse.masks import make_identity
+
+FLOPS = 2 * 1024 * 1024 * 512
+
+F32 = mybir.dt.float32
+BF16 = mybir.dt.bfloat16
+U32 = mybir.dt.uint32
+U8 = mybir.dt.uint8
+FP8X4 = mybir.dt.float8_e4m3fn_x4
+ALU = mybir.AluOpType
+ACT = mybir.ActivationFunctionType
+AX = mybir.AxisListType
+
+P = 128
+NT = 8
+NV = 7
+N = 1024
+C = 512
+BANK = 512
+LO = 64
+HI = 960
+INV = 1.0 / 512.0 ** 0.5
+THR = 0.2
+
+
+def tile_coarsematching_kernel(tc, feat_c0, feat_c1, temperature, out_0, out_1):
+    nc = tc.nc
+    with ExitStack() as ctx:
+        keep = ctx.enter_context(tc.tile_pool(name="keep", bufs=1))
+        work = ctx.enter_context(tc.tile_pool(name="work", bufs=3))
+        psw = ctx.enter_context(tc.psum_pool(name="psw", bufs=3))
+        pss = ctx.enter_context(tc.psum_pool(name="pss", bufs=1))
+        ctx.enter_context(tc.manual_schedule())
+
+        def ptile(n, shape, dt, nm):
+            if n % 4 == 3:
+                return pss.tile(shape, dt, tag="sa", name=nm)
+            return psw.tile(shape, dt, tag="wa", name=nm)
+
+        f0 = feat_c0.flatten_outer_dims()
+        f1 = feat_c1.flatten_outer_dims()
+        o0 = out_0.flatten_outer_dims()
+        o1 = out_1.flatten_outer_dims()
+        o0m = o0[LO:HI, :].rearrange("(i p) s -> p i s", p=P)
+        o1m = o1[LO:HI, :].rearrange("(i p) s -> p i s", p=P)
+
+        raw = [[keep.tile([P, 2, C], BF16, name="raw%d%d" % (a, q)) for q in range(4)] for a in range(2)]
+        f0m = f0[LO:HI, :].rearrange("(i p) c -> p i c", p=P)
+        f1m = f1.rearrange("(i p) c -> p i c", p=P)
+        t_bf = keep.tile([P, 1], BF16)
+        nc.scalar.dma_start(out=t_bf[:], in_=temperature.partition_broadcast(P))
+        for q in range(3):
+            nc.sync.dma_start(out=raw[0][q][:], in_=f0m[:, 2 * q : 2 * q + 2, :])
+        nc.sync.dma_start(out=raw[0][3][:, 0, :], in_=f0m[:, 6, :])
+        nc.sync.dma_start(out=raw[0][3][0:64, 1, :], in_=f0[0:LO, :])
+        nc.sync.dma_start(out=raw[0][3][64:128, 1, :], in_=f0[HI:N, :])
+        for q in range(4):
+            nc.sync.dma_start(out=raw[1][q][:], in_=f1m[:, 2 * q : 2 * q + 2, :])
+
+        ident = keep.tile([P, P], F32)
+        make_identity(nc, ident[:])
+        z8 = keep.tile([P, NT], F32)
+        nc.vector.memset(z8[:], 0.0)
+        c0col = keep.tile([P, 1], F32)
+        nc.scalar.activation(out=c0col[:], in_=z8[:, 0:1], func=ACT.Exp)
+        vf = keep.tile([P, P], F32)
+        nc.vector.memset(vf[:], 1.0)
+        vf3 = vf[:].rearrange("q (a w) -> q a w", w=32)
+        nc.vector.memset(vf3[:, :, 0:2], 0.0)
+        nc.vector.memset(vf3[:, :, 30:32], 0.0)
+        mcs = [keep.tile([P, N], F32, name="mc%d" % k) for k in range(4)]
+        nc.vector.memset(mcs[0][:], 0.0)
+        nc.sync.dma_start(out=o1[0:LO, :], in_=mcs[0][0:64, :])
+        nc.sync.dma_start(out=o1[HI:N, :], in_=mcs[0][64:128, :])
+        vt = pss.tile([P, P], F32, tag="sa")
+        nc.tensor.transpose(vt[:], vf[:], ident[:])
+        valid = keep.tile([P, NV], F32)
+        nc.vector.tensor_copy(out=valid[:], in_=vt[:, 0:NV])
+        tcol = keep.tile([P, 1], F32)
+        nc.vector.tensor_copy(out=tcol[:], in_=t_bf[:])
+        t2col = keep.tile([P, 1], F32)
+        nc.vector.tensor_scalar(out=t2col[:], in0=t_bf[:], scalar1=2.0, scalar2=None, op0=ALU.mult)
+
+        grp = [[keep.tile([P, 4, P, 4], BF16, align_bytes=64, name="g%d%d" % (a, h)) for h in range(2)] for a in range(2)]
+        cod = [[keep.tile([P, BANK], U32, align_bytes=64, name="cod%d%d" % (a, h)) for h in range(2)] for a in range(2)]
+        pl = [[keep.tile([P, BANK], U8, align_bytes=64, name="pl%d%d" % (a, h)) for h in range(2)] for a in range(2)]
+
+        def flip(a, q, n):
+            xt = ptile(n, [P, 2, 2, P], F32, "xt")
+            for r in range(2):
+                for u in range(2):
+                    nc.tensor.transpose(xt[:, r, u, :], raw[a][q][:].bitcast(F32)[:, r, P * u : P * u + P], ident[:])
+            r0 = 2 * (q % 2)
+            nc.scalar.copy(out=grp[a][q // 2][:, r0 : r0 + 2, :, :].bitcast(F32), in_=xt[:].rearrange("p i u r -> p i r u"))
+
+        def scale(a, h):
+            gv = grp[a][h][:].rearrange("p i r t -> p (i r t)")
+            nc.vector.tensor_scalar(out=gv, in0=gv, scalar1=INV, scalar2=None, op0=ALU.mult)
+
+        def quant(a, h):
+            nc.vector.quantize_mx(out=cod[a][h][:].bitcast(FP8X4), scales=pl[a][h][:],
+                                  in_=grp[a][h][:].rearrange("p i r t -> p (i r t)"))
+
+        for a in range(2):
+            for q in range(4):
+                flip(a, q, 4 * a + q)
+        scale(0, 0)
+        scale(0, 1)
+        quant(0, 0)
+        scale(1, 0)
+        quant(0, 1)
+        scale(1, 1)
+        quant(1, 0)
+        quant(1, 1)
+
+        def sim_pass(out, stat, j, mov, h):
+            c = slice(P * (j % 4), P * (j % 4) + P)
+            nc.tensor.matmul_mx(
+                out=out,
+                lhsT=cod[stat][j // 4][:, c].bitcast(FP8X4),
+                lhsT_scale=pl[stat][j // 4][:, c],
+                rhs=cod[mov][h][:].bitcast(FP8X4),
+                rhs_scale=pl[mov][h][:],
+                start=True,
+                stop=True,
+            )
+
+        xb = [keep.tile([P, N], F32, name="xb%d" % j) for j in range(NT)]
+        nmbs = [keep.tile([P, 1], F32, name="nmb%d" % j) for j in range(NT)]
+        mb2 = keep.tile([P, 2 * NT], F32)
+        nmb = keep.tile([P, NT], F32)
+        cs = keep.tile([P, NT], F32)
+        junk = keep.tile([P, N], BF16)
+        for j in range(NT):
+            sb = ptile(j, [P, N], F32, "sb")
+            for h in range(2):
+                hs = slice(BANK * h, BANK * h + BANK)
+                sim_pass(sb[:, hs], 1, j, 0, h)
+                nc.vector.tensor_scalar(out=xb[j][:, hs], in0=sb[:, hs], scalar1=t2col[:, 0:1], scalar2=None,
+                                        op0=ALU.mult, op1=ALU.max, accum_out=mb2[:, 2 * j + h : 2 * j + h + 1])
+            nc.vector.tensor_scalar(out=nmbs[j][:], in0=mb2[:, 2 * j : 2 * j + 1],
+                                    scalar1=mb2[:, 2 * j + 1 : 2 * j + 2], scalar2=-0.5, op0=ALU.max, op1=ALU.mult)
+            nc.vector.tensor_scalar(out=nmb[:, j : j + 1], in0=mb2[:, 2 * j : 2 * j + 1],
+                                    scalar1=mb2[:, 2 * j + 1 : 2 * j + 2], scalar2=-0.5, op0=ALU.max, op1=ALU.mult)
+            nc.scalar.activation(out=junk[:], in_=xb[j][:], func=ACT.Exp, bias=nmbs[j][:], scale=0.5,
+                                 accum_out=cs[:, j : j + 1])
+        lncs = keep.tile([P, NT], F32)
+        nc.scalar.activation(out=lncs[:], in_=cs[:], func=ACT.Ln)
+        dummy = keep.tile([P, NT], F32)
+        nc.scalar.activation(out=dummy[:], in_=z8[:], func=ACT.Exp)
+        run = keep.tile([P, HI - LO], F32)
+        nc.vector.memset(run[:], 0.0)
+        for k in range(1, 4):
+            nc.vector.memset(mcs[k][:], 0.0)
+        nb = keep.tile([P, NT], F32)
+        nc.vector.tensor_tensor(out=nb[:], in0=nmb[:], in1=lncs[:], op=ALU.subtract)
+        nbrep = keep.tile([P, NT, P], F32)
+        nc.vector.tensor_copy(out=nbrep[:], in_=nb[:].unsqueeze(2).to_broadcast([P, NT, P]))
+
+        conf = [keep.tile([P, N], F32, name="conf%d" % i) for i in range(NT)]
+        w2 = keep.tile([P, 2 * NT], F32)
+        nws = [keep.tile([P, 1], F32, name="nw%d" % i) for i in range(NT)]
+        rs2 = [keep.tile([P, 2], F32, name="rs%d" % i) for i in range(NT)]
+        rsum = keep.tile([P, NT], F32)
+        ras = [keep.tile([P, 1], F32, name="ra%d" % i) for i in range(NT)]
+        rmx = keep.tile([P, NT], F32)
+        was = {}
+        sas = {}
+
+        def make_sa(i):
+            sa = pss.tile([P, N], F32, tag="sa", name="sa")
+            for h in range(2):
+                sim_pass(sa[:, BANK * h : BANK * h + BANK], 0, i, 1, h)
+            sas[i] = sa
+
+        def make_wa(i):
+            wa = psw.tile([P, N], F32, tag="wa", name="wa")
+            for j in range(NT):
+                nc.tensor.matmul(wa[:, P * j : P * j + P], lhsT=xb[j][:, P * i : P * i + P], rhs=ident[:],
+                                 is_transpose=True, start=True, stop=False)
+                nc.tensor.matmul(wa[:, P * j : P * j + P], lhsT=nbrep[:, j, :], rhs=ident[:],
+                                 is_transpose=True, start=False, stop=True)
+            was[i] = wa
+
+        def row_max(i):
+            for h in range(2):
+                nc.vector.tensor_reduce(out=w2[:, 2 * i + h : 2 * i + h + 1], in_=was[i][:, BANK * h : BANK * h + BANK],
+                                        axis=AX.X, op=ALU.max)
+            nc.vector.tensor_scalar(out=nws[i][:], in0=w2[:, 2 * i : 2 * i + 1],
+                                    scalar1=w2[:, 2 * i + 1 : 2 * i + 2], scalar2=-1.0, op0=ALU.max, op1=ALU.mult)
+
+        def exps(i):
+            for h in range(2):
+                nc.scalar.activation(out=junk[:, BANK * h : BANK * h + BANK], in_=sas[i][:, BANK * h : BANK * h + BANK],
+                                     func=ACT.Exp, bias=nws[i][:], scale=tcol[:, 0:1], accum_out=rs2[i][:, h : h + 1])
+            for h in range(2):
+                hs = slice(BANK * h, BANK * h + BANK)
+                nc.scalar.activation(out=conf[i][:, hs], in_=was[i][:, hs], func=ACT.Exp, bias=nws[i][:], scale=1.0)
+
+        def norm(i):
+            nc.vector.tensor_tensor(out=rsum[:, i : i + 1], in0=rs2[i][:, 0:1], in1=rs2[i][:, 1:2], op=ALU.add)
+            nc.vector.reciprocal(out=ras[i][:], in_=rsum[:, i : i + 1])
+            nc.gpsimd.tensor_scalar(out=conf[i][:], in0=conf[i][:], scalar1=ras[i][:], scalar2=1.0,
+                                    op0=ALU.mult, op1=ALU.mult)
+            nc.gpsimd.tensor_scalar(out=rmx[:, i : i + 1], in0=c0col[:], scalar1=ras[i][:], scalar2=1.0,
+                                    op0=ALU.mult, op1=ALU.mult)
+            if i < NV:
+                nc.sync.dma_start(out=o0m[:, i, :], in_=conf[i][:])
+            else:
+                nc.sync.dma_start(out=o0[0:LO, :], in_=conf[i][0:64, :])
+                nc.sync.dma_start(out=o0[HI:N, :], in_=conf[i][64:128, :])
+
+        def inner(ap):
+            return ap.rearrange("p (g w) -> p g w", w=32)[:, :, 2:30]
+
+        def col_max(i):
+            if i == 1:
+                nc.vector.tensor_tensor(out=inner(run[:]), in0=inner(conf[0][:, LO:HI]), in1=inner(conf[1][:, LO:HI]),
+                                        op=ALU.max)
+            elif i > 1:
+                nc.vector.tensor_tensor(out=inner(run[:]), in0=inner(run[:]), in1=inner(conf[i][:, LO:HI]), op=ALU.max)
+
+        make_sa(0)
+        make_wa(0)
+        make_wa(1)
+        row_max(0)
+        for i in range(NT):
+            exps(i)
+            if i + 1 < NT:
+                row_max(i + 1)
+            if i + 2 < NT:
+                make_wa(i + 2)
+            if i + 1 < NT:
+                make_sa(i + 1)
+            norm(i)
+            if i >= 1:
+                col_max(i - 1)
+
+        def guarded(dst, mx, nm):
+            ok = keep.tile([P, NV], F32, name="ok" + nm)
+            nc.vector.scalar_tensor_tensor(out=ok[:], in0=mx, scalar=THR, in1=valid[:], op0=ALU.is_gt, op1=ALU.mult)
+            nc.vector.tensor_scalar(out=ok[:], in0=ok[:], scalar1=-2.0, scalar2=2.0, op0=ALU.mult, op1=ALU.add)
+            nc.vector.tensor_tensor(out=dst[:], in0=mx, in1=ok[:], op=ALU.max)
+
+        rmp = keep.tile([P, NV], F32)
+        guarded(rmp, rmx[:, 0:NV], "r")
+        col_max(NT - 1)
+        cmt = psw.tile([P, NV, P], F32, tag="wa")
+        for b in range(NV):
+            nc.tensor.transpose(cmt[:, b, :], run[:, P * b : P * b + P], ident[:])
+        cmx = keep.tile([P, NV], F32)
+        nc.vector.tensor_reduce(out=cmx[:, 0:4], in_=cmt[:, 0:4, :], axis=AX.X, op=ALU.max)
+        nc.vector.tensor_reduce(out=cmx[:, 4:NV], in_=cmt[:, 4:NV, :], axis=AX.X, op=ALU.max)
+        cmp = keep.tile([P, NV], F32)
+        guarded(cmp, cmx[:], "c")
+        bc = keep.tile([P, NV, P], F32)
+        nc.vector.tensor_copy(out=bc[:], in_=cmp[:].unsqueeze(2).to_broadcast([P, NV, P]))
+        cb = psw.tile([P, HI - LO], F32, tag="wa")
+        for b in range(NV):
+            nc.tensor.transpose(cb[:, P * b : P * b + P], bc[:, b, :], ident[:])
+
+        for i in range(NV):
+            mask = work.tile([P, 28 * 28], F32, tag="mask")
+            nc.vector.scalar_tensor_tensor(
+                out=mask[:, 0:448].rearrange("p (g w) -> p g w", w=28), in0=inner(cb[:, 0:BANK]),
+                scalar=rmp[:, i : i + 1], in1=inner(conf[i][:, LO : LO + BANK]), op0=ALU.max, op1=ALU.is_le)
+            nc.vector.scalar_tensor_tensor(
+                out=mask[:, 448:784].rearrange("p (g w) -> p g w", w=28), in0=inner(cb[:, BANK : HI - LO]),
+                scalar=rmp[:, i : i + 1], in1=inner(conf[i][:, LO + BANK : HI]), op0=ALU.max, op1=ALU.is_le)
+            mc = mcs[i % 4]
+            m3 = mask[:].rearrange("p (g w) -> p g w", w=28)
+            if i % 2 == 0:
+                nc.scalar.activation(out=inner(mc[:, LO:HI]), in_=m3, func=ACT.Copy, scale=rmp[:, i : i + 1])
+            else:
+                nc.gpsimd.tensor_scalar(out=inner(mc[:, LO:HI]), in0=m3, scalar1=rmp[:, i : i + 1], scalar2=1.0,
+                                        op0=ALU.mult, op1=ALU.mult)
+            nc.sync.dma_start(out=o1m[:, i, :], in_=mc[:])

@@ -77,8 +77,8 @@ def tile_coarsematching_kernel(tc, feat_c0, feat_c1, temperature, out_0, out_1):
         nc.sync.dma_start(out=o1[HI:N, :], in_=mcs[0][64:128, :])
         vt = pss.tile([P, P], F32, tag="sa")
         nc.tensor.transpose(vt[:], vf[:], ident[:])
-        valid = keep.tile([P, NV], F32)
-        nc.vector.tensor_copy(out=valid[:], in_=vt[:, 0:NV])
+        inv2 = keep.tile([P, 1], F32)
+        nc.vector.tensor_scalar(out=inv2[:], in0=vt[:, 0:1], scalar1=-2.0, scalar2=2.0, op0=ALU.mult, op1=ALU.add)
         tcol = keep.tile([P, 1], F32)
         nc.vector.tensor_copy(out=tcol[:], in_=t_bf[:])
         t2col = keep.tile([P, 1], F32)
@@ -112,9 +112,7 @@ def tile_coarsematching_kernel(tc, feat_c0, feat_c1, temperature, out_0, out_1):
         quant(0, 0)
         scale(1, 0)
         quant(0, 1)
-        scale(1, 1)
         quant(1, 0)
-        quant(1, 1)
 
         def sim_pass(out, stat, j, mov, h):
             c = slice(P * (j % 4), P * (j % 4) + P)
@@ -129,11 +127,17 @@ def tile_coarsematching_kernel(tc, feat_c0, feat_c1, temperature, out_0, out_1):
             )
 
         xb = [keep.tile([P, N], F32, name="xb%d" % j) for j in range(NT)]
-        nmbs = [keep.tile([P, 1], F32, name="nmb%d" % j) for j in range(NT)]
         mb2 = keep.tile([P, 2 * NT], F32)
         nmb = keep.tile([P, NT], F32)
         cs = keep.tile([P, NT], F32)
         junk = keep.tile([P, N], BF16)
+
+        def col_shift(j):
+            nc.vector.tensor_scalar(out=nmb[:, j : j + 1], in0=mb2[:, 2 * j : 2 * j + 1],
+                                    scalar1=mb2[:, 2 * j + 1 : 2 * j + 2], scalar2=-0.5, op0=ALU.max, op1=ALU.mult)
+            nc.scalar.activation(out=junk[:], in_=xb[j][:], func=ACT.Exp, bias=nmb[:, j : j + 1], scale=0.5,
+                                 accum_out=cs[:, j : j + 1])
+
         for j in range(NT):
             sb = ptile(j, [P, N], F32, "sb")
             for h in range(2):
@@ -141,12 +145,13 @@ def tile_coarsematching_kernel(tc, feat_c0, feat_c1, temperature, out_0, out_1):
                 sim_pass(sb[:, hs], 1, j, 0, h)
                 nc.vector.tensor_scalar(out=xb[j][:, hs], in0=sb[:, hs], scalar1=t2col[:, 0:1], scalar2=None,
                                         op0=ALU.mult, op1=ALU.max, accum_out=mb2[:, 2 * j + h : 2 * j + h + 1])
-            nc.vector.tensor_scalar(out=nmbs[j][:], in0=mb2[:, 2 * j : 2 * j + 1],
-                                    scalar1=mb2[:, 2 * j + 1 : 2 * j + 2], scalar2=-0.5, op0=ALU.max, op1=ALU.mult)
-            nc.vector.tensor_scalar(out=nmb[:, j : j + 1], in0=mb2[:, 2 * j : 2 * j + 1],
-                                    scalar1=mb2[:, 2 * j + 1 : 2 * j + 2], scalar2=-0.5, op0=ALU.max, op1=ALU.mult)
-            nc.scalar.activation(out=junk[:], in_=xb[j][:], func=ACT.Exp, bias=nmbs[j][:], scale=0.5,
-                                 accum_out=cs[:, j : j + 1])
+                if h == 0 and j > 0:
+                    col_shift(j - 1)
+            if j == 0:
+                scale(1, 1)
+            if j == 1:
+                quant(1, 1)
+        col_shift(NT - 1)
         lncs = keep.tile([P, NT], F32)
         nc.scalar.activation(out=lncs[:], in_=cs[:], func=ACT.Ln)
         dummy = keep.tile([P, NT], F32)
@@ -157,10 +162,9 @@ def tile_coarsematching_kernel(tc, feat_c0, feat_c1, temperature, out_0, out_1):
             nc.vector.memset(mcs[k][:], 0.0)
         nb = keep.tile([P, NT], F32)
         nc.vector.tensor_tensor(out=nb[:], in0=nmb[:], in1=lncs[:], op=ALU.subtract)
-        nbrep = keep.tile([P, NT, P], F32)
-        nc.vector.tensor_copy(out=nbrep[:], in_=nb[:].unsqueeze(2).to_broadcast([P, NT, P]))
 
         conf = [keep.tile([P, N], F32, name="conf%d" % i) for i in range(NT)]
+        last = keep.tile([P, N], F32)
         w2 = keep.tile([P, 2 * NT], F32)
         nws = [keep.tile([P, 1], F32, name="nw%d" % i) for i in range(NT)]
         rs2 = [keep.tile([P, 2], F32, name="rs%d" % i) for i in range(NT)]
@@ -181,14 +185,17 @@ def tile_coarsematching_kernel(tc, feat_c0, feat_c1, temperature, out_0, out_1):
             for j in range(NT):
                 nc.tensor.matmul(wa[:, P * j : P * j + P], lhsT=xb[j][:, P * i : P * i + P], rhs=ident[:],
                                  is_transpose=True, start=True, stop=False)
-                nc.tensor.matmul(wa[:, P * j : P * j + P], lhsT=nbrep[:, j, :], rhs=ident[:],
+                nc.tensor.matmul(wa[:, P * j : P * j + P], lhsT=nb[:, j : j + 1].to_broadcast([P, P]), rhs=ident[:],
                                  is_transpose=True, start=False, stop=True)
             was[i] = wa
 
         def row_max(i):
             for h in range(2):
-                nc.vector.tensor_reduce(out=w2[:, 2 * i + h : 2 * i + h + 1], in_=was[i][:, BANK * h : BANK * h + BANK],
-                                        axis=AX.X, op=ALU.max)
+                hs = slice(BANK * h, BANK * h + BANK)
+                nc.vector.tensor_scalar(out=conf[i][:, hs], in0=was[i][:, hs], scalar1=1.0, scalar2=None,
+                                        op0=ALU.mult, op1=ALU.max, accum_out=w2[:, 2 * i + h : 2 * i + h + 1])
+
+        def row_shift(i):
             nc.vector.tensor_scalar(out=nws[i][:], in0=w2[:, 2 * i : 2 * i + 1],
                                     scalar1=w2[:, 2 * i + 1 : 2 * i + 2], scalar2=-1.0, op0=ALU.max, op1=ALU.mult)
 
@@ -196,22 +203,23 @@ def tile_coarsematching_kernel(tc, feat_c0, feat_c1, temperature, out_0, out_1):
             for h in range(2):
                 nc.scalar.activation(out=junk[:, BANK * h : BANK * h + BANK], in_=sas[i][:, BANK * h : BANK * h + BANK],
                                      func=ACT.Exp, bias=nws[i][:], scale=tcol[:, 0:1], accum_out=rs2[i][:, h : h + 1])
-            for h in range(2):
-                hs = slice(BANK * h, BANK * h + BANK)
-                nc.scalar.activation(out=conf[i][:, hs], in_=was[i][:, hs], func=ACT.Exp, bias=nws[i][:], scale=1.0)
+            nc.scalar.activation(out=conf[i][:], in_=conf[i][:], func=ACT.Exp, bias=nws[i][:], scale=1.0)
+
+        def row_sum(i):
+            nc.vector.tensor_tensor(out=rsum[:, i : i + 1], in0=rs2[i][:, 0:1], in1=rs2[i][:, 1:2], op=ALU.add)
 
         def norm(i):
-            nc.vector.tensor_tensor(out=rsum[:, i : i + 1], in0=rs2[i][:, 0:1], in1=rs2[i][:, 1:2], op=ALU.add)
             nc.vector.reciprocal(out=ras[i][:], in_=rsum[:, i : i + 1])
-            nc.gpsimd.tensor_scalar(out=conf[i][:], in0=conf[i][:], scalar1=ras[i][:], scalar2=1.0,
-                                    op0=ALU.mult, op1=ALU.mult)
-            nc.gpsimd.tensor_scalar(out=rmx[:, i : i + 1], in0=c0col[:], scalar1=ras[i][:], scalar2=1.0,
+            dst = conf[i] if i < NV else last
+            nc.gpsimd.tensor_scalar(out=dst[:], in0=conf[i][:], scalar1=ras[i][:], scalar2=1.0,
                                     op0=ALU.mult, op1=ALU.mult)
             if i < NV:
+                nc.gpsimd.tensor_scalar(out=rmx[:, i : i + 1], in0=c0col[:], scalar1=ras[i][:], scalar2=1.0,
+                                        op0=ALU.mult, op1=ALU.mult)
                 nc.sync.dma_start(out=o0m[:, i, :], in_=conf[i][:])
             else:
-                nc.sync.dma_start(out=o0[0:LO, :], in_=conf[i][0:64, :])
-                nc.sync.dma_start(out=o0[HI:N, :], in_=conf[i][64:128, :])
+                nc.sync.dma_start(out=o0[0:LO, :], in_=last[0:64, :])
+                nc.sync.dma_start(out=o0[HI:N, :], in_=last[64:128, :])
 
         def inner(ap):
             return ap.rearrange("p (g w) -> p g w", w=32)[:, :, 2:30]
@@ -220,6 +228,9 @@ def tile_coarsematching_kernel(tc, feat_c0, feat_c1, temperature, out_0, out_1):
             if i == 1:
                 nc.vector.tensor_tensor(out=inner(run[:]), in0=inner(conf[0][:, LO:HI]), in1=inner(conf[1][:, LO:HI]),
                                         op=ALU.max)
+            elif i == NT - 1:
+                nc.vector.scalar_tensor_tensor(out=inner(run[:]), in0=inner(conf[i][:, LO:HI]), scalar=ras[i][:],
+                                               in1=inner(run[:]), op0=ALU.mult, op1=ALU.max)
             elif i > 1:
                 nc.vector.tensor_tensor(out=inner(run[:]), in0=inner(run[:]), in1=inner(conf[i][:, LO:HI]), op=ALU.max)
 
@@ -227,6 +238,7 @@ def tile_coarsematching_kernel(tc, feat_c0, feat_c1, temperature, out_0, out_1):
         make_wa(0)
         make_wa(1)
         row_max(0)
+        row_shift(0)
         for i in range(NT):
             exps(i)
             if i + 1 < NT:
@@ -235,40 +247,41 @@ def tile_coarsematching_kernel(tc, feat_c0, feat_c1, temperature, out_0, out_1):
                 make_wa(i + 2)
             if i + 1 < NT:
                 make_sa(i + 1)
+            row_sum(i)
+            if i + 1 < NT:
+                row_shift(i + 1)
             norm(i)
             if i >= 1:
                 col_max(i - 1)
 
-        def guarded(dst, mx, nm):
-            ok = keep.tile([P, NV], F32, name="ok" + nm)
-            nc.vector.scalar_tensor_tensor(out=ok[:], in0=mx, scalar=THR, in1=valid[:], op0=ALU.is_gt, op1=ALU.mult)
-            nc.vector.tensor_scalar(out=ok[:], in0=ok[:], scalar1=-2.0, scalar2=2.0, op0=ALU.mult, op1=ALU.add)
-            nc.vector.tensor_tensor(out=dst[:], in0=mx, in1=ok[:], op=ALU.max)
-
-        rmp = keep.tile([P, NV], F32)
-        guarded(rmp, rmx[:, 0:NV], "r")
+        low = keep.tile([P, NV], F32)
+        nc.vector.tensor_scalar(out=low[:], in0=rmx[:, 0:NV], scalar1=THR, scalar2=2.0, op0=ALU.is_le, op1=ALU.mult)
         col_max(NT - 1)
-        cmt = psw.tile([P, NV, P], F32, tag="wa")
-        for b in range(NV):
-            nc.tensor.transpose(cmt[:, b, :], run[:, P * b : P * b + P], ident[:])
+        rmp = keep.tile([P, NV], F32)
+        nc.vector.scalar_tensor_tensor(out=rmp[:], in0=low[:], scalar=inv2[:], in1=rmx[:, 0:NV], op0=ALU.max, op1=ALU.max)
+        split = [(0, 4), (4, NV)]
         cmx = keep.tile([P, NV], F32)
-        nc.vector.tensor_reduce(out=cmx[:, 0:4], in_=cmt[:, 0:4, :], axis=AX.X, op=ALU.max)
-        nc.vector.tensor_reduce(out=cmx[:, 4:NV], in_=cmt[:, 4:NV, :], axis=AX.X, op=ALU.max)
-        cmp = keep.tile([P, NV], F32)
-        guarded(cmp, cmx[:], "c")
-        bc = keep.tile([P, NV, P], F32)
-        nc.vector.tensor_copy(out=bc[:], in_=cmp[:].unsqueeze(2).to_broadcast([P, NV, P]))
-        cb = psw.tile([P, HI - LO], F32, tag="wa")
-        for b in range(NV):
-            nc.tensor.transpose(cb[:, P * b : P * b + P], bc[:, b, :], ident[:])
+        cmts = []
+        for n, (b0, b1) in enumerate(split):
+            cmt = psw.tile([P, b1 - b0, P], F32, tag="wa", name="cmt")
+            for b in range(b0, b1):
+                nc.tensor.transpose(cmt[:, b - b0, :], run[:, P * b : P * b + P], ident[:])
+            cmts.append(cmt)
+        cbs = []
+        for n, (b0, b1) in enumerate(split):
+            nc.vector.tensor_reduce(out=cmx[:, b0:b1], in_=cmts[n][:], axis=AX.X, op=ALU.max)
+            cb = ptile(2 + n, [P, (b1 - b0) * P], F32, "cb")
+            for b in range(b0, b1):
+                nc.tensor.transpose(cb[:, P * (b - b0) : P * (b - b0) + P], cmx[:, b : b + 1].to_broadcast([P, P]), ident[:])
+            cbs.append(cb)
 
         for i in range(NV):
             mask = work.tile([P, 28 * 28], F32, tag="mask")
             nc.vector.scalar_tensor_tensor(
-                out=mask[:, 0:448].rearrange("p (g w) -> p g w", w=28), in0=inner(cb[:, 0:BANK]),
+                out=mask[:, 0:448].rearrange("p (g w) -> p g w", w=28), in0=inner(cbs[0][:]),
                 scalar=rmp[:, i : i + 1], in1=inner(conf[i][:, LO : LO + BANK]), op0=ALU.max, op1=ALU.is_le)
             nc.vector.scalar_tensor_tensor(
-                out=mask[:, 448:784].rearrange("p (g w) -> p g w", w=28), in0=inner(cb[:, BANK : HI - LO]),
+                out=mask[:, 448:784].rearrange("p (g w) -> p g w", w=28), in0=inner(cbs[1][:]),
                 scalar=rmp[:, i : i + 1], in1=inner(conf[i][:, LO + BANK : HI]), op0=ALU.max, op1=ALU.is_le)
             mc = mcs[i % 4]
             m3 = mask[:].rearrange("p (g w) -> p g w", w=28)

@@ -71,10 +71,16 @@ def tile_coarsematching_kernel(tc, feat_c0, feat_c1, temperature, out_0, out_1):
         vf3 = vf[:].rearrange("q (a w) -> q a w", w=32)
         nc.vector.memset(vf3[:, :, 0:2], 0.0)
         nc.vector.memset(vf3[:, :, 30:32], 0.0)
-        mcs = [keep.tile([P, N], F32, name="mc%d" % k) for k in range(4)]
-        nc.vector.memset(mcs[0][:], 0.0)
-        nc.sync.dma_start(out=o1[0:LO, :], in_=mcs[0][0:64, :])
-        nc.sync.dma_start(out=o1[HI:N, :], in_=mcs[0][64:128, :])
+        mcs = [keep.tile([P, HI - LO], F32, name="mc%d" % k) for k in range(NV)]
+        for k in range(4, NV):
+            nc.gpsimd.memset(mcs[k][:], 0.0)
+        zero = keep.tile([P, N], F32)
+        nc.vector.memset(zero[:], 0.0)
+        nc.sync.dma_start(out=o1[0:LO, :], in_=zero[0:64, :])
+        nc.sync.dma_start(out=o1[HI:N, :], in_=zero[64:128, :])
+        zside = zero[:, 0 : NV * LO].rearrange("p (i s) -> p i s", s=LO)
+        nc.sync.dma_start(out=o1m[:, :, 0:LO], in_=zside)
+        nc.sync.dma_start(out=o1m[:, :, HI:N], in_=zside)
         vt = pss.tile([P, P], F32, tag="sa")
         nc.tensor.transpose(vt[:], vf[:], ident[:])
         inv2 = keep.tile([P, 1], F32)
@@ -100,6 +106,10 @@ def tile_coarsematching_kernel(tc, feat_c0, feat_c1, temperature, out_0, out_1):
             gv = grp[a][h][:].rearrange("p i r t -> p (i r t)")
             nc.vector.tensor_scalar(out=gv, in0=gv, scalar1=INV, scalar2=None, op0=ALU.mult)
 
+        def scale_on_scalar(a, h):
+            gv = grp[a][h][:].rearrange("p i r t -> p (i r t)")
+            nc.scalar.activation(out=gv, in_=gv, func=ACT.Copy, scale=INV)
+
         def quant(a, h):
             nc.vector.quantize_mx(out=cod[a][h][:].bitcast(FP8X4), scales=pl[a][h][:],
                                   in_=grp[a][h][:].rearrange("p i r t -> p (i r t)"))
@@ -113,6 +123,7 @@ def tile_coarsematching_kernel(tc, feat_c0, feat_c1, temperature, out_0, out_1):
         scale(1, 0)
         quant(0, 1)
         quant(1, 0)
+        scale_on_scalar(1, 1)
 
         def sim_pass(out, stat, j, mov, h):
             c = slice(P * (j % 4), P * (j % 4) + P)
@@ -133,7 +144,7 @@ def tile_coarsematching_kernel(tc, feat_c0, feat_c1, temperature, out_0, out_1):
         junk = keep.tile([P, N], BF16)
 
         def col_shift(j):
-            nc.vector.tensor_scalar(out=nmb[:, j : j + 1], in0=mb2[:, 2 * j : 2 * j + 1],
+            nc.gpsimd.tensor_scalar(out=nmb[:, j : j + 1], in0=mb2[:, 2 * j : 2 * j + 1],
                                     scalar1=mb2[:, 2 * j + 1 : 2 * j + 2], scalar2=-0.5, op0=ALU.max, op1=ALU.mult)
             nc.scalar.activation(out=junk[:], in_=xb[j][:], func=ACT.Exp, bias=nmb[:, j : j + 1], scale=0.5,
                                  accum_out=cs[:, j : j + 1])
@@ -145,23 +156,28 @@ def tile_coarsematching_kernel(tc, feat_c0, feat_c1, temperature, out_0, out_1):
                 sim_pass(sb[:, hs], 1, j, 0, h)
                 nc.vector.tensor_scalar(out=xb[j][:, hs], in0=sb[:, hs], scalar1=t2col[:, 0:1], scalar2=None,
                                         op0=ALU.mult, op1=ALU.max, accum_out=mb2[:, 2 * j + h : 2 * j + h + 1])
-                if h == 0 and j > 0:
-                    col_shift(j - 1)
-            if j == 0:
-                scale(1, 1)
+            col_shift(j)
             if j == 1:
                 quant(1, 1)
-        col_shift(NT - 1)
         lncs = keep.tile([P, NT], F32)
         nc.scalar.activation(out=lncs[:], in_=cs[:], func=ACT.Ln)
-        dummy = keep.tile([P, NT], F32)
-        nc.scalar.activation(out=dummy[:], in_=z8[:], func=ACT.Exp)
         run = keep.tile([P, HI - LO], F32)
         nc.vector.memset(run[:], 0.0)
-        for k in range(1, 4):
+        for k in range(4):
             nc.vector.memset(mcs[k][:], 0.0)
         nb = keep.tile([P, NT], F32)
         nc.vector.tensor_tensor(out=nb[:], in0=nmb[:], in1=lncs[:], op=ALU.subtract)
+        late = slice(BANK, N)
+        for j in (0, 1):
+            nc.vector.tensor_scalar(out=xb[j][:, late], in0=xb[j][:, late], scalar1=nb[:, j : j + 1], scalar2=None,
+                                    op0=ALU.add)
+        for j in (2, 3, 4, 5):
+            nc.gpsimd.tensor_scalar(out=xb[j][:, late], in0=xb[j][:, late], scalar1=nb[:, j : j + 1], scalar2=1.0,
+                                    op0=ALU.add, op1=ALU.mult)
+        for j in (6, 7):
+            nc.scalar.activation(out=xb[j][:, late], in_=xb[j][:, late], func=ACT.Identity, bias=nb[:, j : j + 1], scale=1.0)
+        dummy = keep.tile([P, NT], F32)
+        nc.scalar.activation(out=dummy[:], in_=z8[:], func=ACT.Exp)
 
         conf = [keep.tile([P, N], F32, name="conf%d" % i) for i in range(NT)]
         last = keep.tile([P, N], F32)
@@ -180,14 +196,22 @@ def tile_coarsematching_kernel(tc, feat_c0, feat_c1, temperature, out_0, out_1):
                 sim_pass(sa[:, BANK * h : BANK * h + BANK], 0, i, 1, h)
             sas[i] = sa
 
-        def make_wa(i):
+        def wa_x(i):
             wa = psw.tile([P, N], F32, tag="wa", name="wa")
             for j in range(NT):
                 nc.tensor.matmul(wa[:, P * j : P * j + P], lhsT=xb[j][:, P * i : P * i + P], rhs=ident[:],
-                                 is_transpose=True, start=True, stop=False)
-                nc.tensor.matmul(wa[:, P * j : P * j + P], lhsT=nb[:, j : j + 1].to_broadcast([P, P]), rhs=ident[:],
-                                 is_transpose=True, start=False, stop=True)
+                                 is_transpose=True, start=(j % 4 == 0), stop=(i >= 4 and j % 4 == 3))
             was[i] = wa
+
+        def wa_nb(i):
+            for j in range(NT):
+                nc.tensor.matmul(was[i][:, P * j : P * j + P], lhsT=nb[:, j : j + 1].to_broadcast([P, P]), rhs=ident[:],
+                                 is_transpose=True, start=False, stop=(j % 4 == 3))
+
+        def make_wa(i):
+            wa_x(i)
+            if i < 4:
+                wa_nb(i)
 
         def row_max(i):
             for h in range(2):
@@ -203,7 +227,9 @@ def tile_coarsematching_kernel(tc, feat_c0, feat_c1, temperature, out_0, out_1):
             for h in range(2):
                 nc.scalar.activation(out=junk[:, BANK * h : BANK * h + BANK], in_=sas[i][:, BANK * h : BANK * h + BANK],
                                      func=ACT.Exp, bias=nws[i][:], scale=tcol[:, 0:1], accum_out=rs2[i][:, h : h + 1])
-            nc.scalar.activation(out=conf[i][:], in_=conf[i][:], func=ACT.Exp, bias=nws[i][:], scale=1.0)
+            cuts = [(0, N)] if i < NT - 1 else [(0, LO + BANK), (LO + BANK, N)]
+            for c0, c1 in cuts:
+                nc.scalar.activation(out=conf[i][:, c0:c1], in_=conf[i][:, c0:c1], func=ACT.Exp, bias=nws[i][:], scale=1.0)
 
         def row_sum(i):
             nc.vector.tensor_tensor(out=rsum[:, i : i + 1], in0=rs2[i][:, 0:1], in1=rs2[i][:, 1:2], op=ALU.add)
@@ -229,22 +255,25 @@ def tile_coarsematching_kernel(tc, feat_c0, feat_c1, temperature, out_0, out_1):
                 nc.vector.tensor_tensor(out=inner(run[:]), in0=inner(conf[0][:, LO:HI]), in1=inner(conf[1][:, LO:HI]),
                                         op=ALU.max)
             elif i == NT - 1:
-                nc.vector.scalar_tensor_tensor(out=inner(run[:]), in0=inner(conf[i][:, LO:HI]), scalar=ras[i][:],
-                                               in1=inner(run[:]), op0=ALU.mult, op1=ALU.max)
+                for c0, c1 in ((0, BANK), (BANK, HI - LO)):
+                    nc.vector.scalar_tensor_tensor(out=inner(run[:, c0:c1]), in0=inner(conf[i][:, LO + c0 : LO + c1]),
+                                                   scalar=ras[i][:], in1=inner(run[:, c0:c1]), op0=ALU.mult, op1=ALU.max)
             elif i > 1:
                 nc.vector.tensor_tensor(out=inner(run[:]), in0=inner(run[:]), in1=inner(conf[i][:, LO:HI]), op=ALU.max)
 
         make_sa(0)
-        make_wa(0)
-        make_wa(1)
+        for i in range(3):
+            wa_x(i)
+        for i in range(3):
+            wa_nb(i)
         row_max(0)
         row_shift(0)
         for i in range(NT):
             exps(i)
             if i + 1 < NT:
                 row_max(i + 1)
-            if i + 2 < NT:
-                make_wa(i + 2)
+            if i + 3 < NT:
+                make_wa(i + 3)
             if i + 1 < NT:
                 make_sa(i + 1)
             row_sum(i)
@@ -283,11 +312,14 @@ def tile_coarsematching_kernel(tc, feat_c0, feat_c1, temperature, out_0, out_1):
             nc.vector.scalar_tensor_tensor(
                 out=mask[:, 448:784].rearrange("p (g w) -> p g w", w=28), in0=inner(cbs[1][:]),
                 scalar=rmp[:, i : i + 1], in1=inner(conf[i][:, LO + BANK : HI]), op0=ALU.max, op1=ALU.is_le)
-            mc = mcs[i % 4]
-            m3 = mask[:].rearrange("p (g w) -> p g w", w=28)
-            if i % 2 == 0:
-                nc.scalar.activation(out=inner(mc[:, LO:HI]), in_=m3, func=ACT.Copy, scale=rmp[:, i : i + 1])
-            else:
-                nc.gpsimd.tensor_scalar(out=inner(mc[:, LO:HI]), in0=m3, scalar1=rmp[:, i : i + 1], scalar2=1.0,
-                                        op0=ALU.mult, op1=ALU.mult)
-            nc.sync.dma_start(out=o1m[:, i, :], in_=mc[:])
+            mc = mcs[i]
+            nc.scalar.activation(out=inner(mc[:, 0:BANK]), in_=mask[:, 0:448].rearrange("p (g w) -> p g w", w=28),
+                                 func=ACT.Copy, scale=rmp[:, i : i + 1])
+            if i == 0:
+                nc.sync.dma_start(out=o1m[:, i, LO : LO + BANK], in_=mc[:, 0:BANK])
+            nc.gpsimd.tensor_scalar(out=inner(mc[:, BANK : HI - LO]), in0=mask[:, 448:784].rearrange("p (g w) -> p g w", w=28),
+                                    scalar1=rmp[:, i : i + 1], scalar2=1.0, op0=ALU.mult, op1=ALU.mult)
+            if i == 0:
+                nc.sync.dma_start(out=o1m[:, i, LO + BANK : HI], in_=mc[:, BANK : HI - LO])
+                continue
+            nc.sync.dma_start(out=o1m[:, i, LO:HI], in_=mc[:])

@@ -168,14 +168,9 @@ def tile_coarsematching_kernel(tc, feat_c0, feat_c1, temperature, out_0, out_1):
         nb = keep.tile([P, NT], F32)
         nc.vector.tensor_tensor(out=nb[:], in0=nmb[:], in1=lncs[:], op=ALU.subtract)
         late = slice(BANK, N)
-        for j in (0, 1):
-            nc.vector.tensor_scalar(out=xb[j][:, late], in0=xb[j][:, late], scalar1=nb[:, j : j + 1], scalar2=None,
-                                    op0=ALU.add)
-        for j in (2, 3, 4, 5):
+        for j in range(NT):
             nc.gpsimd.tensor_scalar(out=xb[j][:, late], in0=xb[j][:, late], scalar1=nb[:, j : j + 1], scalar2=1.0,
                                     op0=ALU.add, op1=ALU.mult)
-        for j in (6, 7):
-            nc.scalar.activation(out=xb[j][:, late], in_=xb[j][:, late], func=ACT.Identity, bias=nb[:, j : j + 1], scale=1.0)
         dummy = keep.tile([P, NT], F32)
         nc.scalar.activation(out=dummy[:], in_=z8[:], func=ACT.Exp)
 

@@ -44,21 +44,27 @@ def tile_coarsematching_kernel(tc, feat_c0, feat_c1, temperature, out_0, out_1):
         f1 = feat_c1.flatten_outer_dims()
         o0 = out_0.flatten_outer_dims()
         o1 = out_1.flatten_outer_dims()
-        o0m = o0[LO:HI, :].rearrange("(i p) s -> p i s", p=P)
         o1m = o1[LO:HI, :].rearrange("(i p) s -> p i s", p=P)
+        MID = LO + 6 * P
+
+        def rows_of(ap, i):
+            if i < 6:
+                return ap[LO:MID, :].rearrange("(q p e) s -> q e p s", p=P, e=2)[i // 2, i % 2]
+            return ap[MID:HI, :]
 
         raw = [[keep.tile([P, 2, C], BF16, name="raw%d%d" % (a, q)) for q in range(4)] for a in range(2)]
-        f0m = f0[LO:HI, :].rearrange("(i p) c -> p i c", p=P)
-        f1m = f1.rearrange("(i p) c -> p i c", p=P)
-        t_bf = keep.tile([P, 1], BF16)
-        nc.scalar.dma_start(out=t_bf[:], in_=temperature.partition_broadcast(P))
+        f0m = f0[LO:MID, :].rearrange("(q p e) c -> q p e c", p=P, e=2)
+        f1m = f1.rearrange("(q p e) c -> q p e c", p=P, e=2)
+        trow = keep.tile([P, 32], BF16)
+        nc.vector.memset(trow[:], 0.0)
+        nc.scalar.dma_start(out=trow[0:1, 0:1], in_=temperature.rearrange("(o t) -> o t", o=1))
         for q in range(3):
-            nc.sync.dma_start(out=raw[0][q][:], in_=f0m[:, 2 * q : 2 * q + 2, :])
-        nc.sync.dma_start(out=raw[0][3][:, 0, :], in_=f0m[:, 6, :])
+            nc.sync.dma_start(out=raw[0][q][:], in_=f0m[q])
+        nc.sync.dma_start(out=raw[0][3][:, 0, :], in_=f0[MID:HI, :])
         nc.sync.dma_start(out=raw[0][3][0:64, 1, :], in_=f0[0:LO, :])
         nc.sync.dma_start(out=raw[0][3][64:128, 1, :], in_=f0[HI:N, :])
         for q in range(4):
-            nc.sync.dma_start(out=raw[1][q][:], in_=f1m[:, 2 * q : 2 * q + 2, :])
+            nc.sync.dma_start(out=raw[1][q][:], in_=f1m[q])
 
         ident = keep.tile([P, P], F32)
         make_identity(nc, ident[:])
@@ -66,11 +72,16 @@ def tile_coarsematching_kernel(tc, feat_c0, feat_c1, temperature, out_0, out_1):
         nc.vector.memset(z8[:], 0.0)
         c0col = keep.tile([P, 1], F32)
         nc.scalar.activation(out=c0col[:], in_=z8[:, 0:1], func=ACT.Exp)
-        vf = keep.tile([P, P], F32)
-        nc.vector.memset(vf[:], 1.0)
-        vf3 = vf[:].rearrange("q (a w) -> q a w", w=32)
-        nc.vector.memset(vf3[:, :, 0:2], 0.0)
-        nc.vector.memset(vf3[:, :, 30:32], 0.0)
+        vf = keep.tile([P, 2, P], F32)
+        nc.vector.memset(vf[:], 0.0)
+        va = vf[:, 0, :].rearrange("q (a w) -> q a w", w=16)
+        nc.vector.memset(va[:, :, 0:1], 1.0)
+        nc.vector.memset(va[:, :, 15:16], 1.0)
+        vb = vf[:, 1, :].rearrange("q (a w) -> q a w", w=32)
+        nc.vector.memset(vb[:, :, 0:2], 1.0)
+        nc.vector.memset(vb[:, :, 30:32], 1.0)
+        ones = keep.tile([P, P], BF16)
+        nc.vector.memset(ones[:], 1.0)
         mcs = [keep.tile([P, HI - LO], F32, name="mc%d" % k) for k in range(NV)]
         for k in range(4, NV):
             nc.gpsimd.memset(mcs[k][:], 0.0)
@@ -81,14 +92,14 @@ def tile_coarsematching_kernel(tc, feat_c0, feat_c1, temperature, out_0, out_1):
         zside = zero[:, 0 : NV * LO].rearrange("p (i s) -> p i s", s=LO)
         nc.sync.dma_start(out=o1m[:, :, 0:LO], in_=zside)
         nc.sync.dma_start(out=o1m[:, :, HI:N], in_=zside)
-        vt = pss.tile([P, P], F32, tag="sa")
-        nc.tensor.transpose(vt[:], vf[:], ident[:])
-        inv2 = keep.tile([P, 1], F32)
-        nc.vector.tensor_scalar(out=inv2[:], in0=vt[:, 0:1], scalar1=-2.0, scalar2=2.0, op0=ALU.mult, op1=ALU.add)
+        vt = pss.tile([P, 2, P], F32, tag="sa")
+        for n in range(2):
+            nc.tensor.transpose(vt[:, n, :], vf[:, n, :], ident[:])
+        edge = keep.tile([P, NV], F32)
+        nc.vector.tensor_copy(out=edge[:, 0:6], in_=vt[:, 0, 0:6])
+        nc.vector.tensor_copy(out=edge[:, 6:NV], in_=vt[:, 1, 0:1])
         tcol = keep.tile([P, 1], F32)
-        nc.vector.tensor_copy(out=tcol[:], in_=t_bf[:])
         t2col = keep.tile([P, 1], F32)
-        nc.vector.tensor_scalar(out=t2col[:], in0=t_bf[:], scalar1=2.0, scalar2=None, op0=ALU.mult)
 
         grp = [[keep.tile([P, 4, P, 4], BF16, align_bytes=64, name="g%d%d" % (a, h)) for h in range(2)] for a in range(2)]
         cod = [[keep.tile([P, BANK], U32, align_bytes=64, name="cod%d%d" % (a, h)) for h in range(2)] for a in range(2)]
@@ -100,7 +111,12 @@ def tile_coarsematching_kernel(tc, feat_c0, feat_c1, temperature, out_0, out_1):
                 for u in range(2):
                     nc.tensor.transpose(xt[:, r, u, :], raw[a][q][:].bitcast(F32)[:, r, P * u : P * u + P], ident[:])
             r0 = 2 * (q % 2)
-            nc.scalar.copy(out=grp[a][q // 2][:, r0 : r0 + 2, :, :].bitcast(F32), in_=xt[:].rearrange("p i u r -> p i r u"))
+            dst = grp[a][q // 2][:, r0 : r0 + 2, :, :].bitcast(F32)
+            if a == 0:
+                nc.scalar.copy(out=dst, in_=xt[:].rearrange("p i u r -> p i r u"))
+            else:
+                nc.scalar.copy(out=dst.rearrange("p i r u -> p (i r u)").rearrange("p (r i u) -> p r i u", i=2, u=2),
+                               in_=xt[:].rearrange("p i u r -> p r i u"))
 
         def scale(a, h):
             gv = grp[a][h][:].rearrange("p i r t -> p (i r t)")
@@ -114,9 +130,14 @@ def tile_coarsematching_kernel(tc, feat_c0, feat_c1, temperature, out_0, out_1):
             nc.vector.quantize_mx(out=cod[a][h][:].bitcast(FP8X4), scales=pl[a][h][:],
                                   in_=grp[a][h][:].rearrange("p i r t -> p (i r t)"))
 
-        for a in range(2):
-            for q in range(4):
-                flip(a, q, 4 * a + q)
+        for q in range(4):
+            flip(0, q, q)
+        tt = psw.tile([P, 32], F32, tag="wa")
+        nc.tensor.matmul(tt[:], lhsT=ones[:], rhs=trow[:], start=True, stop=True)
+        nc.vector.tensor_copy(out=tcol[:], in_=tt[:, 0:1])
+        nc.vector.tensor_scalar(out=t2col[:], in0=tt[:, 0:1], scalar1=2.0, scalar2=None, op0=ALU.mult)
+        for q in range(4):
+            flip(1, q, 5 + q)
         scale(0, 0)
         scale(0, 1)
         quant(0, 0)
@@ -150,7 +171,7 @@ def tile_coarsematching_kernel(tc, feat_c0, feat_c1, temperature, out_0, out_1):
                                  accum_out=cs[:, j : j + 1])
 
         for j in range(NT):
-            sb = ptile(j, [P, N], F32, "sb")
+            sb = ptile(j + 1, [P, N], F32, "sb")
             for h in range(2):
                 hs = slice(BANK * h, BANK * h + BANK)
                 sim_pass(sb[:, hs], 1, j, 0, h)
@@ -168,9 +189,14 @@ def tile_coarsematching_kernel(tc, feat_c0, feat_c1, temperature, out_0, out_1):
         nb = keep.tile([P, NT], F32)
         nc.vector.tensor_tensor(out=nb[:], in0=nmb[:], in1=lncs[:], op=ALU.subtract)
         late = slice(BANK, N)
-        for j in range(NT):
+        for j in (0, 1):
+            nc.vector.tensor_scalar(out=xb[j][:, late], in0=xb[j][:, late], scalar1=nb[:, j : j + 1], scalar2=None,
+                                    op0=ALU.add)
+        for j in (2, 3, 4, 5):
             nc.gpsimd.tensor_scalar(out=xb[j][:, late], in0=xb[j][:, late], scalar1=nb[:, j : j + 1], scalar2=1.0,
                                     op0=ALU.add, op1=ALU.mult)
+        for j in (6, 7):
+            nc.scalar.activation(out=xb[j][:, late], in_=xb[j][:, late], func=ACT.Identity, bias=nb[:, j : j + 1], scale=1.0)
         dummy = keep.tile([P, NT], F32)
         nc.scalar.activation(out=dummy[:], in_=z8[:], func=ACT.Exp)
 
@@ -237,7 +263,7 @@ def tile_coarsematching_kernel(tc, feat_c0, feat_c1, temperature, out_0, out_1):
             if i < NV:
                 nc.gpsimd.tensor_scalar(out=rmx[:, i : i + 1], in0=c0col[:], scalar1=ras[i][:], scalar2=1.0,
                                         op0=ALU.mult, op1=ALU.mult)
-                nc.sync.dma_start(out=o0m[:, i, :], in_=conf[i][:])
+                nc.sync.dma_start(out=rows_of(o0, i), in_=conf[i][:])
             else:
                 nc.sync.dma_start(out=o0[0:LO, :], in_=last[0:64, :])
                 nc.sync.dma_start(out=o0[HI:N, :], in_=last[64:128, :])
@@ -278,11 +304,11 @@ def tile_coarsematching_kernel(tc, feat_c0, feat_c1, temperature, out_0, out_1):
             if i >= 1:
                 col_max(i - 1)
 
-        low = keep.tile([P, NV], F32)
-        nc.vector.tensor_scalar(out=low[:], in0=rmx[:, 0:NV], scalar1=THR, scalar2=2.0, op0=ALU.is_le, op1=ALU.mult)
+        bad = keep.tile([P, NV], F32)
+        nc.vector.scalar_tensor_tensor(out=bad[:], in0=rmx[:, 0:NV], scalar=THR, in1=edge[:], op0=ALU.is_le, op1=ALU.max)
         col_max(NT - 1)
         rmp = keep.tile([P, NV], F32)
-        nc.vector.scalar_tensor_tensor(out=rmp[:], in0=low[:], scalar=inv2[:], in1=rmx[:, 0:NV], op0=ALU.max, op1=ALU.max)
+        nc.vector.scalar_tensor_tensor(out=rmp[:], in0=bad[:], scalar=2.0, in1=rmx[:, 0:NV], op0=ALU.mult, op1=ALU.max)
         split = [(0, 4), (4, NV)]
         cmx = keep.tile([P, NV], F32)
         cmts = []
@@ -311,10 +337,10 @@ def tile_coarsematching_kernel(tc, feat_c0, feat_c1, temperature, out_0, out_1):
             nc.scalar.activation(out=inner(mc[:, 0:BANK]), in_=mask[:, 0:448].rearrange("p (g w) -> p g w", w=28),
                                  func=ACT.Copy, scale=rmp[:, i : i + 1])
             if i == 0:
-                nc.sync.dma_start(out=o1m[:, i, LO : LO + BANK], in_=mc[:, 0:BANK])
+                nc.sync.dma_start(out=rows_of(o1, i)[:, LO : LO + BANK], in_=mc[:, 0:BANK])
             nc.gpsimd.tensor_scalar(out=inner(mc[:, BANK : HI - LO]), in0=mask[:, 448:784].rearrange("p (g w) -> p g w", w=28),
                                     scalar1=rmp[:, i : i + 1], scalar2=1.0, op0=ALU.mult, op1=ALU.mult)
             if i == 0:
-                nc.sync.dma_start(out=o1m[:, i, LO + BANK : HI], in_=mc[:, BANK : HI - LO])
+                nc.sync.dma_start(out=rows_of(o1, i)[:, LO + BANK : HI], in_=mc[:, BANK : HI - LO])
                 continue
-            nc.sync.dma_start(out=o1m[:, i, LO:HI], in_=mc[:])
+            nc.sync.dma_start(out=rows_of(o1, i)[:, LO:HI], in_=mc[:])

@@ -31,14 +31,12 @@ def tile_coarsematching_kernel(tc, feat_c0, feat_c1, temperature, out_0, out_1):
     with ExitStack() as ctx:
         keep = ctx.enter_context(tc.tile_pool(name="keep", bufs=1))
         work = ctx.enter_context(tc.tile_pool(name="work", bufs=3))
-        psw = ctx.enter_context(tc.psum_pool(name="psw", bufs=3))
-        pss = ctx.enter_context(tc.psum_pool(name="pss", bufs=1))
+        psw = ctx.enter_context(tc.psum_pool(name="psw", bufs=6))
+        pss = ctx.enter_context(tc.psum_pool(name="pss", bufs=2))
         ctx.enter_context(tc.manual_schedule())
 
-        def ptile(n, shape, dt, nm):
-            if n % 4 == 3:
-                return pss.tile(shape, dt, tag="sa", name=nm)
-            return psw.tile(shape, dt, tag="wa", name=nm)
+        def wtile(shape, nm):
+            return psw.tile(shape, F32, tag="w", name=nm)
 
         f0 = feat_c0.flatten_outer_dims()
         f1 = feat_c1.flatten_outer_dims()
@@ -92,7 +90,7 @@ def tile_coarsematching_kernel(tc, feat_c0, feat_c1, temperature, out_0, out_1):
         zside = zero[:, 0 : NV * LO].rearrange("p (i s) -> p i s", s=LO)
         nc.sync.dma_start(out=o1m[:, :, 0:LO], in_=zside)
         nc.sync.dma_start(out=o1m[:, :, HI:N], in_=zside)
-        vt = pss.tile([P, 2, P], F32, tag="sa")
+        vt = wtile([P, 2, P], "vt")
         for n in range(2):
             nc.tensor.transpose(vt[:, n, :], vf[:, n, :], ident[:])
         edge = keep.tile([P, NV], F32)
@@ -105,8 +103,8 @@ def tile_coarsematching_kernel(tc, feat_c0, feat_c1, temperature, out_0, out_1):
         cod = [[keep.tile([P, BANK], U32, align_bytes=64, name="cod%d%d" % (a, h)) for h in range(2)] for a in range(2)]
         pl = [[keep.tile([P, BANK], U8, align_bytes=64, name="pl%d%d" % (a, h)) for h in range(2)] for a in range(2)]
 
-        def flip(a, q, n):
-            xt = ptile(n, [P, 2, 2, P], F32, "xt")
+        def flip(a, q):
+            xt = wtile([P, 2, 2, P], "xt")
             for r in range(2):
                 for u in range(2):
                     nc.tensor.transpose(xt[:, r, u, :], raw[a][q][:].bitcast(F32)[:, r, P * u : P * u + P], ident[:])
@@ -131,13 +129,13 @@ def tile_coarsematching_kernel(tc, feat_c0, feat_c1, temperature, out_0, out_1):
                                   in_=grp[a][h][:].rearrange("p i r t -> p (i r t)"))
 
         for q in range(4):
-            flip(0, q, q)
-        tt = psw.tile([P, 32], F32, tag="wa")
+            flip(0, q)
+        tt = wtile([P, 32], "tt")
         nc.tensor.matmul(tt[:], lhsT=ones[:], rhs=trow[:], start=True, stop=True)
         nc.vector.tensor_copy(out=tcol[:], in_=tt[:, 0:1])
         nc.vector.tensor_scalar(out=t2col[:], in0=tt[:, 0:1], scalar1=2.0, scalar2=None, op0=ALU.mult)
         for q in range(4):
-            flip(1, q, 5 + q)
+            flip(1, q)
         scale(0, 0)
         scale(0, 1)
         quant(0, 0)
@@ -171,11 +169,11 @@ def tile_coarsematching_kernel(tc, feat_c0, feat_c1, temperature, out_0, out_1):
                                  accum_out=cs[:, j : j + 1])
 
         for j in range(NT):
-            sb = ptile(j + 1, [P, N], F32, "sb")
             for h in range(2):
                 hs = slice(BANK * h, BANK * h + BANK)
-                sim_pass(sb[:, hs], 1, j, 0, h)
-                nc.vector.tensor_scalar(out=xb[j][:, hs], in0=sb[:, hs], scalar1=t2col[:, 0:1], scalar2=None,
+                sb = wtile([P, BANK], "sb")
+                sim_pass(sb[:], 1, j, 0, h)
+                nc.vector.tensor_scalar(out=xb[j][:, hs], in0=sb[:], scalar1=t2col[:, 0:1], scalar2=None,
                                         op0=ALU.mult, op1=ALU.max, accum_out=mb2[:, 2 * j + h : 2 * j + h + 1])
             col_shift(j)
             if j == 1:
@@ -202,31 +200,33 @@ def tile_coarsematching_kernel(tc, feat_c0, feat_c1, temperature, out_0, out_1):
 
         conf = [keep.tile([P, N], F32, name="conf%d" % i) for i in range(NT)]
         last = keep.tile([P, N], F32)
-        w2 = keep.tile([P, 2 * NT], F32)
+        w2 = keep.tile([P, NT], F32)
         nws = [keep.tile([P, 1], F32, name="nw%d" % i) for i in range(NT)]
         rs2 = [keep.tile([P, 2], F32, name="rs%d" % i) for i in range(NT)]
         rsum = keep.tile([P, NT], F32)
-        ras = [keep.tile([P, 1], F32, name="ra%d" % i) for i in range(NT)]
-        rmx = keep.tile([P, NT], F32)
+        ra = keep.tile([P, NT], F32)
+        rmx = keep.tile([P, NV], F32)
         was = {}
         sas = {}
 
         def make_sa(i):
-            sa = pss.tile([P, N], F32, tag="sa", name="sa")
+            sas[i] = []
             for h in range(2):
-                sim_pass(sa[:, BANK * h : BANK * h + BANK], 0, i, 1, h)
-            sas[i] = sa
+                sa = pss.tile([P, BANK], F32, tag="s", name="sa")
+                sim_pass(sa[:], 0, i, 1, h)
+                sas[i].append(sa)
 
         def wa_x(i):
-            wa = psw.tile([P, N], F32, tag="wa", name="wa")
+            was[i] = [wtile([P, BANK], "wa0"), wtile([P, BANK], "wa1")]
             for j in range(NT):
-                nc.tensor.matmul(wa[:, P * j : P * j + P], lhsT=xb[j][:, P * i : P * i + P], rhs=ident[:],
+                c = P * (j % 4)
+                nc.tensor.matmul(was[i][j // 4][:, c : c + P], lhsT=xb[j][:, P * i : P * i + P], rhs=ident[:],
                                  is_transpose=True, start=(j % 4 == 0), stop=(i >= 4 and j % 4 == 3))
-            was[i] = wa
 
         def wa_nb(i):
             for j in range(NT):
-                nc.tensor.matmul(was[i][:, P * j : P * j + P], lhsT=nb[:, j : j + 1].to_broadcast([P, P]), rhs=ident[:],
+                c = P * (j % 4)
+                nc.tensor.matmul(was[i][j // 4][:, c : c + P], lhsT=nb[:, j : j + 1].to_broadcast([P, P]), rhs=ident[:],
                                  is_transpose=True, start=False, stop=(j % 4 == 3))
 
         def make_wa(i):
@@ -234,35 +234,29 @@ def tile_coarsematching_kernel(tc, feat_c0, feat_c1, temperature, out_0, out_1):
             if i < 4:
                 wa_nb(i)
 
-        def row_max(i):
-            for h in range(2):
-                hs = slice(BANK * h, BANK * h + BANK)
-                nc.vector.tensor_scalar(out=conf[i][:, hs], in0=was[i][:, hs], scalar1=1.0, scalar2=None,
-                                        op0=ALU.mult, op1=ALU.max, accum_out=w2[:, 2 * i + h : 2 * i + h + 1])
-
-        def row_shift(i):
-            nc.vector.tensor_scalar(out=nws[i][:], in0=w2[:, 2 * i : 2 * i + 1],
-                                    scalar1=w2[:, 2 * i + 1 : 2 * i + 2], scalar2=-1.0, op0=ALU.max, op1=ALU.mult)
+        def row_max(i, h):
+            hs = slice(BANK * h, BANK * h + BANK)
+            nc.vector.tensor_scalar(out=conf[i][:, hs], in0=was[i][h][:], scalar1=-1.0,
+                                    scalar2=(None if h == 0 else w2[:, i : i + 1]), op0=ALU.mult, op1=ALU.min,
+                                    accum_out=(w2[:, i : i + 1] if h == 0 else nws[i][:]))
 
         def exps(i):
             for h in range(2):
-                nc.scalar.activation(out=junk[:, BANK * h : BANK * h + BANK], in_=sas[i][:, BANK * h : BANK * h + BANK],
+                nc.scalar.activation(out=junk[:, BANK * h : BANK * h + BANK], in_=sas[i][h][:],
                                      func=ACT.Exp, bias=nws[i][:], scale=tcol[:, 0:1], accum_out=rs2[i][:, h : h + 1])
             cuts = [(0, N)] if i < NT - 1 else [(0, LO + BANK), (LO + BANK, N)]
             for c0, c1 in cuts:
-                nc.scalar.activation(out=conf[i][:, c0:c1], in_=conf[i][:, c0:c1], func=ACT.Exp, bias=nws[i][:], scale=1.0)
+                nc.scalar.activation(out=conf[i][:, c0:c1], in_=conf[i][:, c0:c1], func=ACT.Exp, bias=nws[i][:], scale=-1.0)
 
         def row_sum(i):
             nc.vector.tensor_tensor(out=rsum[:, i : i + 1], in0=rs2[i][:, 0:1], in1=rs2[i][:, 1:2], op=ALU.add)
 
         def norm(i):
-            nc.vector.reciprocal(out=ras[i][:], in_=rsum[:, i : i + 1])
+            nc.vector.reciprocal(out=ra[:, i : i + 1], in_=rsum[:, i : i + 1])
             dst = conf[i] if i < NV else last
-            nc.gpsimd.tensor_scalar(out=dst[:], in0=conf[i][:], scalar1=ras[i][:], scalar2=1.0,
+            nc.gpsimd.tensor_scalar(out=dst[:], in0=conf[i][:], scalar1=ra[:, i : i + 1], scalar2=1.0,
                                     op0=ALU.mult, op1=ALU.mult)
             if i < NV:
-                nc.gpsimd.tensor_scalar(out=rmx[:, i : i + 1], in0=c0col[:], scalar1=ras[i][:], scalar2=1.0,
-                                        op0=ALU.mult, op1=ALU.mult)
                 nc.sync.dma_start(out=rows_of(o0, i), in_=conf[i][:])
             else:
                 nc.sync.dma_start(out=o0[0:LO, :], in_=last[0:64, :])
@@ -278,7 +272,7 @@ def tile_coarsematching_kernel(tc, feat_c0, feat_c1, temperature, out_0, out_1):
             elif i == NT - 1:
                 for c0, c1 in ((0, BANK), (BANK, HI - LO)):
                     nc.vector.scalar_tensor_tensor(out=inner(run[:, c0:c1]), in0=inner(conf[i][:, LO + c0 : LO + c1]),
-                                                   scalar=ras[i][:], in1=inner(run[:, c0:c1]), op0=ALU.mult, op1=ALU.max)
+                                                   scalar=ra[:, i : i + 1], in1=inner(run[:, c0:c1]), op0=ALU.mult, op1=ALU.max)
             elif i > 1:
                 nc.vector.tensor_tensor(out=inner(run[:]), in0=inner(run[:]), in1=inner(conf[i][:, LO:HI]), op=ALU.max)
 
@@ -287,40 +281,44 @@ def tile_coarsematching_kernel(tc, feat_c0, feat_c1, temperature, out_0, out_1):
             wa_x(i)
         for i in range(3):
             wa_nb(i)
-        row_max(0)
-        row_shift(0)
+        row_max(0, 0)
+        row_max(0, 1)
         for i in range(NT):
             exps(i)
+            if i >= 1:
+                norm(i - 1)
             if i + 1 < NT:
-                row_max(i + 1)
+                row_max(i + 1, 0)
+            if i >= 2:
+                col_max(i - 2)
+            if i + 1 < NT:
+                row_max(i + 1, 1)
             if i + 3 < NT:
                 make_wa(i + 3)
             if i + 1 < NT:
                 make_sa(i + 1)
             row_sum(i)
-            if i + 1 < NT:
-                row_shift(i + 1)
-            norm(i)
-            if i >= 1:
-                col_max(i - 1)
+        nc.gpsimd.tensor_scalar(out=rmx[:], in0=ra[:, 0:NV], scalar1=c0col[:], scalar2=1.0, op0=ALU.mult, op1=ALU.mult)
+        col_max(NT - 2)
+        norm(NT - 1)
 
         bad = keep.tile([P, NV], F32)
-        nc.vector.scalar_tensor_tensor(out=bad[:], in0=rmx[:, 0:NV], scalar=THR, in1=edge[:], op0=ALU.is_le, op1=ALU.max)
+        nc.vector.scalar_tensor_tensor(out=bad[:], in0=rmx[:], scalar=THR, in1=edge[:], op0=ALU.is_le, op1=ALU.max)
         col_max(NT - 1)
         rmp = keep.tile([P, NV], F32)
-        nc.vector.scalar_tensor_tensor(out=rmp[:], in0=bad[:], scalar=2.0, in1=rmx[:, 0:NV], op0=ALU.mult, op1=ALU.max)
+        nc.vector.scalar_tensor_tensor(out=rmp[:], in0=bad[:], scalar=2.0, in1=rmx[:], op0=ALU.mult, op1=ALU.max)
         split = [(0, 4), (4, NV)]
         cmx = keep.tile([P, NV], F32)
         cmts = []
         for n, (b0, b1) in enumerate(split):
-            cmt = psw.tile([P, b1 - b0, P], F32, tag="wa", name="cmt")
+            cmt = wtile([P, b1 - b0, P], "cmt")
             for b in range(b0, b1):
                 nc.tensor.transpose(cmt[:, b - b0, :], run[:, P * b : P * b + P], ident[:])
             cmts.append(cmt)
         cbs = []
         for n, (b0, b1) in enumerate(split):
             nc.vector.tensor_reduce(out=cmx[:, b0:b1], in_=cmts[n][:], axis=AX.X, op=ALU.max)
-            cb = ptile(2 + n, [P, (b1 - b0) * P], F32, "cb")
+            cb = wtile([P, (b1 - b0) * P], "cb")
             for b in range(b0, b1):
                 nc.tensor.transpose(cb[:, P * (b - b0) : P * (b - b0) + P], cmx[:, b : b + 1].to_broadcast([P, P]), ident[:])
             cbs.append(cb)

@@ -187,9 +187,6 @@ def tile_coarsematching_kernel(tc, feat_c0, feat_c1, temperature, out_0, out_1):
         nb = keep.tile([P, NT], F32)
         nc.vector.tensor_tensor(out=nb[:], in0=nmb[:], in1=lncs[:], op=ALU.subtract)
         late = slice(BANK, N)
-        for j in (0, 1):
-            nc.vector.tensor_scalar(out=xb[j][:, late], in0=xb[j][:, late], scalar1=nb[:, j : j + 1], scalar2=None,
-                                    op0=ALU.add)
         for j in (2, 3, 4, 5):
             nc.gpsimd.tensor_scalar(out=xb[j][:, late], in0=xb[j][:, late], scalar1=nb[:, j : j + 1], scalar2=1.0,
                                     op0=ALU.add, op1=ALU.mult)
@@ -283,16 +280,18 @@ def tile_coarsematching_kernel(tc, feat_c0, feat_c1, temperature, out_0, out_1):
             wa_nb(i)
         row_max(0, 0)
         row_max(0, 1)
+        for j in (0, 1):
+            nc.vector.tensor_scalar(out=xb[j][:, late], in0=xb[j][:, late], scalar1=nb[:, j : j + 1], scalar2=None,
+                                    op0=ALU.add)
         for i in range(NT):
             exps(i)
             if i >= 1:
                 norm(i - 1)
             if i + 1 < NT:
                 row_max(i + 1, 0)
+                row_max(i + 1, 1)
             if i >= 2:
                 col_max(i - 2)
-            if i + 1 < NT:
-                row_max(i + 1, 1)
             if i + 3 < NT:
                 make_wa(i + 3)
             if i + 1 < NT:

@@ -290,13 +290,13 @@ def tile_coarsematching_kernel(tc, feat_c0, feat_c1, temperature, out_0, out_1):
             if i + 1 < NT:
                 row_max(i + 1, 0)
                 row_max(i + 1, 1)
+            row_sum(i)
             if i >= 2:
                 col_max(i - 2)
             if i + 3 < NT:
                 make_wa(i + 3)
             if i + 1 < NT:
                 make_sa(i + 1)
-            row_sum(i)
         nc.gpsimd.tensor_scalar(out=rmx[:], in0=ra[:, 0:NV], scalar1=c0col[:], scalar2=1.0, op0=ALU.mult, op1=ALU.mult)
         col_max(NT - 2)
         norm(NT - 1)

from contextlib import ExitStack

import concourse.mybir as mybir
from concourse.masks import make_identity

FLOPS = 2 * 1024 * 1024 * 512

F32 = mybir.dt.float32
BF16 = mybir.dt.bfloat16
U32 = mybir.dt.uint32
U8 = mybir.dt.uint8
FP8X4 = mybir.dt.float8_e4m3fn_x4
ALU = mybir.AluOpType
ACT = mybir.ActivationFunctionType
AX = mybir.AxisListType

P = 128
NT = 8
NV = 7
N = 1024
C = 512
BANK = 512
LO = 64
HI = 960
INV = 1.0 / 512.0 ** 0.5
THR = 0.2


def tile_coarsematching_kernel(tc, feat_c0, feat_c1, temperature, out_0, out_1):
    nc = tc.nc
    with ExitStack() as ctx:
        keep = ctx.enter_context(tc.tile_pool(name="keep", bufs=1))
        work = ctx.enter_context(tc.tile_pool(name="work", bufs=3))
        psw = ctx.enter_context(tc.psum_pool(name="psw", bufs=6))
        pss = ctx.enter_context(tc.psum_pool(name="pss", bufs=2))
        ctx.enter_context(tc.manual_schedule())

        def wtile(shape, nm):
            return psw.tile(shape, F32, tag="w", name=nm)

        f0 = feat_c0.flatten_outer_dims()
        f1 = feat_c1.flatten_outer_dims()
        o0 = out_0.flatten_outer_dims()
        o1 = out_1.flatten_outer_dims()
        o1m = o1[LO:HI, :].rearrange("(i p) s -> p i s", p=P)
        MID = LO + 6 * P

        def rows_of(ap, i):
            if i < 6:
                return ap[LO:MID, :].rearrange("(q p e) s -> q e p s", p=P, e=2)[i // 2, i % 2]
            return ap[MID:HI, :]

        raw = [[keep.tile([P, 2, C], BF16, name="raw%d%d" % (a, q)) for q in range(4)] for a in range(2)]
        f0m = f0[LO:MID, :].rearrange("(q p e) c -> q p e c", p=P, e=2)
        f1m = f1.rearrange("(q p e) c -> q p e c", p=P, e=2)
        trow = keep.tile([P, 32], BF16)
        nc.vector.memset(trow[:], 0.0)
        nc.scalar.dma_start(out=trow[0:1, 0:1], in_=temperature.rearrange("(o t) -> o t", o=1))
        for q in range(3):
            nc.sync.dma_start(out=raw[0][q][:], in_=f0m[q])
        nc.sync.dma_start(out=raw[0][3][:, 0, :], in_=f0[MID:HI, :])
        nc.sync.dma_start(out=raw[0][3][0:64, 1, :], in_=f0[0:LO, :])
        nc.sync.dma_start(out=raw[0][3][64:128, 1, :], in_=f0[HI:N, :])
        for q in range(4):
            nc.sync.dma_start(out=raw[1][q][:], in_=f1m[q])

        ident = keep.tile([P, P], F32)
        make_identity(nc, ident[:])
        z8 = keep.tile([P, NT], F32)
        nc.vector.memset(z8[:], 0.0)
        c0col = keep.tile([P, 1], F32)
        nc.scalar.activation(out=c0col[:], in_=z8[:, 0:1], func=ACT.Exp)
        vf = keep.tile([P, 2, P], F32)
        nc.vector.memset(vf[:], 0.0)
        va = vf[:, 0, :].rearrange("q (a w) -> q a w", w=16)
        nc.vector.memset(va[:, :, 0:1], 1.0)
        nc.vector.memset(va[:, :, 15:16], 1.0)
        vb = vf[:, 1, :].rearrange("q (a w) -> q a w", w=32)
        nc.vector.memset(vb[:, :, 0:2], 1.0)
        nc.vector.memset(vb[:, :, 30:32], 1.0)
        ones = keep.tile([P, P], BF16)
        nc.vector.memset(ones[:], 1.0)
        mcs = [keep.tile([P, HI - LO], F32, name="mc%d" % k) for k in range(NV)]
        for k in range(4, NV):
            nc.gpsimd.memset(mcs[k][:], 0.0)
        zero = keep.tile([P, N], F32)
        nc.vector.memset(zero[:], 0.0)
        nc.sync.dma_start(out=o1[0:LO, :], in_=zero[0:64, :])
        nc.sync.dma_start(out=o1[HI:N, :], in_=zero[64:128, :])
        zside = zero[:, 0 : NV * LO].rearrange("p (i s) -> p i s", s=LO)
        nc.sync.dma_start(out=o1m[:, :, 0:LO], in_=zside)
        nc.sync.dma_start(out=o1m[:, :, HI:N], in_=zside)
        vt = wtile([P, 2, P], "vt")
        for n in range(2):
            nc.tensor.transpose(vt[:, n, :], vf[:, n, :], ident[:])
        edge = keep.tile([P, NV], F32)
        nc.vector.tensor_copy(out=edge[:, 0:6], in_=vt[:, 0, 0:6])
        nc.vector.tensor_copy(out=edge[:, 6:NV], in_=vt[:, 1, 0:1])
        tcol = keep.tile([P, 1], F32)
        t2col = keep.tile([P, 1], F32)

        grp = [[keep.tile([P, 4, P, 4], BF16, align_bytes=64, name="g%d%d" % (a, h)) for h in range(2)] for a in range(2)]
        cod = [[keep.tile([P, BANK], U32, align_bytes=64, name="cod%d%d" % (a, h)) for h in range(2)] for a in range(2)]
        pl = [[keep.tile([P, BANK], U8, align_bytes=64, name="pl%d%d" % (a, h)) for h in range(2)] for a in range(2)]

        def flip(a, q):
            xt = wtile([P, 2, 2, P], "xt")
            for r in range(2):
                for u in range(2):
                    nc.tensor.transpose(xt[:, r, u, :], raw[a][q][:].bitcast(F32)[:, r, P * u : P * u + P], ident[:])
            r0 = 2 * (q % 2)
            dst = grp[a][q // 2][:, r0 : r0 + 2, :, :].bitcast(F32)
            if a == 0:
                nc.scalar.copy(out=dst, in_=xt[:].rearrange("p i u r -> p i r u"))
            else:
                nc.scalar.copy(out=dst.rearrange("p i r u -> p (i r u)").rearrange("p (r i u) -> p r i u", i=2, u=2),
                               in_=xt[:].rearrange("p i u r -> p r i u"))

        def scale(a, h):
            gv = grp[a][h][:].rearrange("p i r t -> p (i r t)")
            nc.vector.tensor_scalar(out=gv, in0=gv, scalar1=INV, scalar2=None, op0=ALU.mult)

        def scale_on_scalar(a, h):
            gv = grp[a][h][:].rearrange("p i r t -> p (i r t)")
            nc.scalar.activation(out=gv, in_=gv, func=ACT.Copy, scale=INV)

        def quant(a, h):
            nc.vector.quantize_mx(out=cod[a][h][:].bitcast(FP8X4), scales=pl[a][h][:],
                                  in_=grp[a][h][:].rearrange("p i r t -> p (i r t)"))

        for q in range(4):
            flip(0, q)
        tt = wtile([P, 32], "tt")
        nc.tensor.matmul(tt[:], lhsT=ones[:], rhs=trow[:], start=True, stop=True)
        nc.vector.tensor_copy(out=tcol[:], in_=tt[:, 0:1])
        nc.vector.tensor_scalar(out=t2col[:], in0=tt[:, 0:1], scalar1=2.0, scalar2=None, op0=ALU.mult)
        for q in range(4):
            flip(1, q)
        scale(0, 0)
        scale(0, 1)
        quant(0, 0)
        scale(1, 0)
        quant(0, 1)
        quant(1, 0)
        scale_on_scalar(1, 1)

        def sim_pass(out, stat, j, mov, h):
            c = slice(P * (j % 4), P * (j % 4) + P)
            nc.tensor.matmul_mx(
                out=out,
                lhsT=cod[stat][j // 4][:, c].bitcast(FP8X4),
                lhsT_scale=pl[stat][j // 4][:, c],
                rhs=cod[mov][h][:].bitcast(FP8X4),
                rhs_scale=pl[mov][h][:],
                start=True,
                stop=True,
            )

        xb = [keep.tile([P, N], F32, name="xb%d" % j) for j in range(NT)]
        mb2 = keep.tile([P, 2 * NT], F32)
        nmb = keep.tile([P, NT], F32)
        cs = keep.tile([P, NT], F32)
        junk = keep.tile([P, N], BF16)

        def col_shift(j):
            nc.gpsimd.tensor_scalar(out=nmb[:, j : j + 1], in0=mb2[:, 2 * j : 2 * j + 1],
                                    scalar1=mb2[:, 2 * j + 1 : 2 * j + 2], scalar2=-0.5, op0=ALU.max, op1=ALU.mult)
            nc.scalar.activation(out=junk[:], in_=xb[j][:], func=ACT.Exp, bias=nmb[:, j : j + 1], scale=0.5,
                                 accum_out=cs[:, j : j + 1])

        for j in range(NT):
            for h in range(2):
                hs = slice(BANK * h, BANK * h + BANK)
                sb = wtile([P, BANK], "sb")
                sim_pass(sb[:], 1, j, 0, h)
                nc.vector.tensor_scalar(out=xb[j][:, hs], in0=sb[:], scalar1=t2col[:, 0:1], scalar2=None,
                                        op0=ALU.mult, op1=ALU.max, accum_out=mb2[:, 2 * j + h : 2 * j + h + 1])
            col_shift(j)
            if j == 1:
                quant(1, 1)
        lncs = keep.tile([P, NT], F32)
        nc.scalar.activation(out=lncs[:], in_=cs[:], func=ACT.Ln)
        run = keep.tile([P, HI - LO], F32)
        nc.vector.memset(run[:], 0.0)
        for k in range(4):
            nc.vector.memset(mcs[k][:], 0.0)
        nb = keep.tile([P, NT], F32)
        nc.vector.tensor_tensor(out=nb[:], in0=nmb[:], in1=lncs[:], op=ALU.subtract)
        late = slice(BANK, N)
        for j in (2, 3, 4, 5):
            nc.gpsimd.tensor_scalar(out=xb[j][:, late], in0=xb[j][:, late], scalar1=nb[:, j : j + 1], scalar2=1.0,
                                    op0=ALU.add, op1=ALU.mult)
        for j in (6, 7):
            nc.scalar.activation(out=xb[j][:, late], in_=xb[j][:, late], func=ACT.Identity, bias=nb[:, j : j + 1], scale=1.0)
        dummy = keep.tile([P, NT], F32)
        nc.scalar.activation(out=dummy[:], in_=z8[:], func=ACT.Exp)

        conf = [keep.tile([P, N], F32, name="conf%d" % i) for i in range(NT)]
        last = keep.tile([P, N], F32)
        w2 = keep.tile([P, NT], F32)
        nws = [keep.tile([P, 1], F32, name="nw%d" % i) for i in range(NT)]
        rs2 = [keep.tile([P, 2], F32, name="rs%d" % i) for i in range(NT)]
        rsum = keep.tile([P, NT], F32)
        ra = keep.tile([P, NT], F32)
        rmx = keep.tile([P, NV], F32)
        was = {}
        sas = {}

        def make_sa(i):
            sas[i] = []
            for h in range(2):
                sa = pss.tile([P, BANK], F32, tag="s", name="sa")
                sim_pass(sa[:], 0, i, 1, h)
                sas[i].append(sa)

        def wa_x(i):
            was[i] = [wtile([P, BANK], "wa0"), wtile([P, BANK], "wa1")]
            for j in range(NT):
                c = P * (j % 4)
                nc.tensor.matmul(was[i][j // 4][:, c : c + P], lhsT=xb[j][:, P * i : P * i + P], rhs=ident[:],
                                 is_transpose=True, start=(j % 4 == 0), stop=(i >= 4 and j % 4 == 3))

        def wa_nb(i):
            for j in range(NT):
                c = P * (j % 4)
                nc.tensor.matmul(was[i][j // 4][:, c : c + P], lhsT=nb[:, j : j + 1].to_broadcast([P, P]), rhs=ident[:],
                                 is_transpose=True, start=False, stop=(j % 4 == 3))

        def make_wa(i):
            wa_x(i)
            if i < 4:
                wa_nb(i)

        def row_max(i, h):
            hs = slice(BANK * h, BANK * h + BANK)
            nc.vector.tensor_scalar(out=conf[i][:, hs], in0=was[i][h][:], scalar1=-1.0,
                                    scalar2=(None if h == 0 else w2[:, i : i + 1]), op0=ALU.mult, op1=ALU.min,
                                    accum_out=(w2[:, i : i + 1] if h == 0 else nws[i][:]))

        def exps(i):
            for h in range(2):
                nc.scalar.activation(out=junk[:, BANK * h : BANK * h + BANK], in_=sas[i][h][:],
                                     func=ACT.Exp, bias=nws[i][:], scale=tcol[:, 0:1], accum_out=rs2[i][:, h : h + 1])
            cuts = [(0, N)] if i < NT - 1 else [(0, LO + BANK), (LO + BANK, N)]
            for c0, c1 in cuts:
                nc.scalar.activation(out=conf[i][:, c0:c1], in_=conf[i][:, c0:c1], func=ACT.Exp, bias=nws[i][:], scale=-1.0)

        def row_sum(i):
            nc.vector.tensor_tensor(out=rsum[:, i : i + 1], in0=rs2[i][:, 0:1], in1=rs2[i][:, 1:2], op=ALU.add)

        def norm(i):
            nc.vector.reciprocal(out=ra[:, i : i + 1], in_=rsum[:, i : i + 1])
            dst = conf[i] if i < NV else last
            nc.gpsimd.tensor_scalar(out=dst[:], in0=conf[i][:], scalar1=ra[:, i : i + 1], scalar2=1.0,
                                    op0=ALU.mult, op1=ALU.mult)
            if i < NV:
                nc.sync.dma_start(out=rows_of(o0, i), in_=conf[i][:])
            else:
                nc.sync.dma_start(out=o0[0:LO, :], in_=last[0:64, :])
                nc.sync.dma_start(out=o0[HI:N, :], in_=last[64:128, :])

        def inner(ap):
            return ap.rearrange("p (g w) -> p g w", w=32)[:, :, 2:30]

        def col_max(i):
            if i == 1:
                nc.vector.tensor_tensor(out=inner(run[:]), in0=inner(conf[0][:, LO:HI]), in1=inner(conf[1][:, LO:HI]),
                                        op=ALU.max)
            elif i == NT - 1:
                for c0, c1 in ((0, BANK), (BANK, HI - LO)):
                    nc.vector.scalar_tensor_tensor(out=inner(run[:, c0:c1]), in0=inner(conf[i][:, LO + c0 : LO + c1]),
                                                   scalar=ra[:, i : i + 1], in1=inner(run[:, c0:c1]), op0=ALU.mult, op1=ALU.max)
            elif i > 1:
                nc.vector.tensor_tensor(out=inner(run[:]), in0=inner(run[:]), in1=inner(conf[i][:, LO:HI]), op=ALU.max)

        make_sa(0)
        for i in range(3):
            wa_x(i)
        for i in range(3):
            wa_nb(i)
        row_max(0, 0)
        row_max(0, 1)
        for j in (0, 1):
            nc.vector.tensor_scalar(out=xb[j][:, late], in0=xb[j][:, late], scalar1=nb[:, j : j + 1], scalar2=None,
                                    op0=ALU.add)
        for i in range(NT):
            exps(i)
            if i >= 1:
                norm(i - 1)
            if i + 1 < NT:
                row_max(i + 1, 0)
                row_max(i + 1, 1)
            row_sum(i)
            if i >= 2:
                col_max(i - 2)
            if i + 3 < NT:
                make_wa(i + 3)
            if i + 1 < NT:
                make_sa(i + 1)
        nc.gpsimd.tensor_scalar(out=rmx[:], in0=ra[:, 0:NV], scalar1=c0col[:], scalar2=1.0, op0=ALU.mult, op1=ALU.mult)
        col_max(NT - 2)
        norm(NT - 1)

        bad = keep.tile([P, NV], F32)
        nc.vector.scalar_tensor_tensor(out=bad[:], in0=rmx[:], scalar=THR, in1=edge[:], op0=ALU.is_le, op1=ALU.max)
        col_max(NT - 1)
        rmp = keep.tile([P, NV], F32)
        nc.vector.scalar_tensor_tensor(out=rmp[:], in0=bad[:], scalar=2.0, in1=rmx[:], op0=ALU.mult, op1=ALU.max)
        split = [(0, 4), (4, NV)]
        cmx = keep.tile([P, NV], F32)
        cmts = []
        for n, (b0, b1) in enumerate(split):
            cmt = wtile([P, b1 - b0, P], "cmt")
            for b in range(b0, b1):
                nc.tensor.transpose(cmt[:, b - b0, :], run[:, P * b : P * b + P], ident[:])
            cmts.append(cmt)
        cbs = []
        for n, (b0, b1) in enumerate(split):
            nc.vector.tensor_reduce(out=cmx[:, b0:b1], in_=cmts[n][:], axis=AX.X, op=ALU.max)
            cb = wtile([P, (b1 - b0) * P], "cb")
            for b in range(b0, b1):
                nc.tensor.transpose(cb[:, P * (b - b0) : P * (b - b0) + P], cmx[:, b : b + 1].to_broadcast([P, P]), ident[:])
            cbs.append(cb)

        for i in range(NV):
            mask = work.tile([P, 28 * 28], F32, tag="mask")
            nc.vector.scalar_tensor_tensor(
                out=mask[:, 0:448].rearrange("p (g w) -> p g w", w=28), in0=inner(cbs[0][:]),
                scalar=rmp[:, i : i + 1], in1=inner(conf[i][:, LO : LO + BANK]), op0=ALU.max, op1=ALU.is_le)
            nc.vector.scalar_tensor_tensor(
                out=mask[:, 448:784].rearrange("p (g w) -> p g w", w=28), in0=inner(cbs[1][:]),
                scalar=rmp[:, i : i + 1], in1=inner(conf[i][:, LO + BANK : HI]), op0=ALU.max, op1=ALU.is_le)
            mc = mcs[i]
            nc.scalar.activation(out=inner(mc[:, 0:BANK]), in_=mask[:, 0:448].rearrange("p (g w) -> p g w", w=28),
                                 func=ACT.Copy, scale=rmp[:, i : i + 1])
            if i == 0:
                nc.sync.dma_start(out=rows_of(o1, i)[:, LO : LO + BANK], in_=mc[:, 0:BANK])
            nc.gpsimd.tensor_scalar(out=inner(mc[:, BANK : HI - LO]), in0=mask[:, 448:784].rearrange("p (g w) -> p g w", w=28),
                                    scalar1=rmp[:, i : i + 1], scalar2=1.0, op0=ALU.mult, op1=ALU.mult)
            if i == 0:
                nc.sync.dma_start(out=rows_of(o1, i)[:, LO + BANK : HI], in_=mc[:, BANK : HI - LO])
                continue
            nc.sync.dma_start(out=rows_of(o1, i)[:, LO:HI], in_=mc[:])
